import numpy as np
import ml_dtypes


def mxq(x, axis, fmt="e4m3"):
    dtype, down = {"e4m3": (ml_dtypes.float8_e4m3fn, 7), "e5m2": (ml_dtypes.float8_e5m2, 14)}[fmt]
    v = np.moveaxis(np.asarray(x, np.float32).astype(ml_dtypes.bfloat16).astype(np.float64), axis, -1)
    blocks = v.reshape(v.shape[:-1] + (-1, 32))
    amax = np.abs(blocks).max(-1, keepdims=True)
    byte = np.maximum(np.where(amax > 0, np.frexp(amax)[1] - 1 + 127, 0) - down, 1)
    scale = np.exp2(byte - 127.0)
    codes = (blocks / scale).astype(np.float32).astype(dtype).astype(np.float64)
    return np.moveaxis((codes * scale).reshape(v.shape), -1, axis)


WIDE = False


def mx_kscale(k):
    if not WIDE:
        return np.ones(k)
    levels = np.array([20, -20, 10, -10, 0])
    if k % 512:
        return np.exp2(np.random.permutation(np.resize(levels, k // 32))).repeat(32)
    a = np.empty((k // 512, 16))
    for p in range(k // 512):
        a[p, :8] = np.random.permutation(np.resize(levels, 8))
        for g in range(8):
            far = levels[np.abs(levels - a[p, g]) >= 10]
            a[p, g + 8] = far[np.random.randint(len(far))]
    return np.exp2(a.ravel()).repeat(32)


BF16 = ml_dtypes.bfloat16


def bf(x):
    return np.asarray(x, np.float32).astype(BF16)


def f64(x):
    return np.asarray(x).astype(np.float64)


NS, NI, T = 512, 128, 4097
NA = NS + NI


def setup_inputs():
    u = mx_kscale(NS)
    A = np.random.standard_normal((NS, NS)) / np.sqrt(NA)
    B = np.random.standard_normal((NS, NI)) / np.sqrt(NA)
    x0 = np.random.standard_normal(NS) * 3.0
    V = np.random.standard_normal((T, NA))
    V[0, :NS] *= 3.0
    g = np.random.standard_normal((T, NS)) * np.exp2(np.random.randint(-12, 1, (T, 1))) * 4.0
    V[:, :NS] = V[:, :NS] / u[None, :]
    return {"A": bf(A * u[None, :] / u[:, None]), "B": bf(B / u[:, None]), "x0": bf(x0 / u),
            "net_input": bf(V.reshape(-1)), "T": T, "grad_out": bf((g * u[None, :]).reshape(-1))}


def reference(A, B, x0, net_input, T, grad_out):
    n_state = A.shape[0]
    n_all = n_state + B.shape[1]
    AB = np.concatenate([f64(A), f64(B)], axis=1)
    G = f64(grad_out).reshape(T, n_state)
    gV = np.zeros((T, n_all))
    gV[:-1] = mxq(G[1:], 1, "e5m2") @ mxq(AB, 0, "e4m3")
    gV[0, :n_state] += G[0]
    gV[1:, :n_state] -= G[1:]
    return gV.reshape(-1)

@@ -1,0 +1,161 @@
+from contextlib import ExitStack
+
+import concourse.mybir as mybir
+from concourse.masks import make_identity
+
+BF16 = mybir.dt.bfloat16
+F32 = mybir.dt.float32
+U32 = mybir.dt.uint32
+U8 = mybir.dt.uint8
+E5M2_X4 = mybir.dt.float8_e5m2_x4
+E4M3_X4 = mybir.dt.float8_e4m3fn_x4
+
+P = 128
+PACK = 4
+NS = 512
+NI = 128
+NA = NS + NI
+STEPS = 4096
+TILES = STEPS // P
+GROUP = 4
+STORE_TILES = 2
+N_GROUPS = TILES // GROUP
+WORDS = NS // 2
+N_PASS = 512
+
+FLOPS = 2 * STEPS * NS * NA
+BYTES = 2 * NS * NA + 2 * (STEPS + 1) * NS + 4 * (STEPS + 1) * NA
+
+
+def tile_constrainnet_t_kernel(tc, A, B, x0, net_input, T, grad_out, out):
+    nc = tc.nc
+    assert T == STEPS + 1
+
+    g_next = grad_out[NS : (STEPS + 1) * NS].rearrange("(p s k) -> p s k", p=P, k=NS)
+    g_first = grad_out[0 : STEPS * NS].rearrange("(p s k) -> p s k", p=P, k=NS)[:, 0, :]
+    g_last = grad_out[STEPS * NS : (STEPS + 1) * NS].rearrange("(o k) -> o k", o=1)
+    d_rows = out[0 : STEPS * NA].rearrange("(p j n) -> p j n", p=P, n=NA)
+    d_last = out[STEPS * NA : (STEPS + 1) * NA].rearrange("(o n) -> o n", o=1)
+
+    with ExitStack() as ctx:
+        ctx.enter_context(tc.manual_schedule())
+        keep = ctx.enter_context(tc.tile_pool(name="keep", bufs=1))
+        stage = ctx.enter_context(tc.tile_pool(name="stage", bufs=2))
+        psum_t = ctx.enter_context(tc.psum_pool(name="psum_t", bufs=2))
+        psum_a = ctx.enter_context(tc.psum_pool(name="psum_a", bufs=3))
+        psum_b = ctx.enter_context(tc.psum_pool(name="psum_b", bufs=3))
+
+        g_sb = keep.tile([P, (TILES + 1) * NS], BF16)
+        g_rows = g_sb[:].rearrange("p (s k) -> p s k", k=NS)
+        g_words = g_sb[:].bitcast(F32).rearrange("p (s w) -> p s w", w=WORDS)
+        g_codes = keep.tile([P, TILES * P], U32, align_bytes=64)
+        g_scales = keep.tile([P, TILES * P], U8, align_bytes=64)
+        a_raw = keep.tile([P, PACK, NS], BF16)
+        b_raw = keep.tile([P, PACK, NI], BF16)
+        ab_grouped = keep.tile([P, NA, PACK], BF16, align_bytes=64)
+        ab_codes = keep.tile([P, NA], U32, align_bytes=64)
+        ab_scales = keep.tile([P, NA], U8, align_bytes=64)
+        d_sb = keep.tile([P, TILES, NA], F32)
+        g_last_sb = keep.tile([1, NS], BF16)
+        d_last_sb = keep.tile([1, NA], F32)
+        identity = keep.tile([P, P], F32)
+
+        def load_weight(raw, weight):
+            nc.sync.dma_start(out=raw[:], in_=weight.rearrange("(q t) n -> q t n", t=PACK))
+
+        def load_group(c):
+            nc.sync.dma_start(
+                out=g_rows[:, 1 + c * GROUP : 1 + (c + 1) * GROUP, :],
+                in_=g_next[:, c * GROUP : (c + 1) * GROUP, :],
+            )
+
+        def regroup_weight(raw, cols):
+            nc.vector.tensor_copy(
+                out=ab_grouped[:, cols, :].rearrange("p (c i) t -> p c t i", i=4),
+                in_=raw[:].rearrange("p t (c i) -> p c t i", i=4),
+            )
+
+        def quantise_weight(cols):
+            nc.vector.quantize_mx(
+                out=ab_codes[:, cols].bitcast(E4M3_X4),
+                scales=ab_scales[:, cols],
+                in_=ab_grouped[:, cols, :].rearrange("p n t -> p (n t)"),
+            )
+
+        def transpose_group(c):
+            grouped = stage.tile([P, GROUP * P * PACK], BF16, align_bytes=64)
+            grouped_words = grouped[:].bitcast(F32).rearrange("p (j r u) -> p j r u", j=GROUP, u=2)
+            for half in range(GROUP // 2):
+                bank = psum_t.tile([P, 2, 2, P], F32)
+                for i in range(2):
+                    s = c * GROUP + 2 * half + i + 1
+                    for u in range(2):
+                        nc.tensor.transpose(
+                            bank[:, i, u, :], g_words[:, s, u:WORDS:2], identity[:]
+                        )
+                nc.scalar.copy(
+                    out=grouped_words[:, 2 * half : 2 * half + 2, :, :],
+                    in_=bank[:].rearrange("p i u r -> p i r u"),
+                )
+            return grouped
+
+        def quantise_group(c, grouped):
+            cols = slice(c * GROUP * P, (c + 1) * GROUP * P)
+            nc.vector.quantize_mx(
+                out=g_codes[:, cols].bitcast(E5M2_X4), scales=g_scales[:, cols], in_=grouped[:]
+            )
+
+        def multiply_tile(j):
+            cols = slice(j * P, (j + 1) * P)
+            acc_a = psum_a.tile([P, N_PASS], F32)
+            acc_b = psum_b.tile([P, N_PASS], F32)
+            for acc, first in ((acc_a, 0), (acc_b, NA - N_PASS)):
+                nc.tensor.matmul_mx(
+                    out=acc[:],
+                    lhsT=g_codes[:, cols].bitcast(E5M2_X4),
+                    lhsT_scale=g_scales[:, cols],
+                    rhs=ab_codes[:, first : first + N_PASS].bitcast(E4M3_X4),
+                    rhs_scale=ab_scales[:, first : first + N_PASS],
+                    start=True,
+                    stop=True,
+                )
+            nc.vector.tensor_tensor(
+                out=d_sb[:, j, 0:NS], in0=acc_a[:], in1=g_rows[:, j, :], op=mybir.AluOpType.subtract
+            )
+            nc.scalar.copy(out=d_sb[:, j, NS:NA], in_=acc_b[:, N_PASS - NI : N_PASS])
+
+        def store_tiles(tiles):
+            nc.sync.dma_start(out=d_rows[:, tiles, :], in_=d_sb[:, tiles, :])
+
+        nc.sync.dma_start(out=g_last_sb[:], in_=g_last)
+        load_weight(a_raw, A)
+        load_group(0)
+        load_weight(b_raw, B)
+        nc.sync.dma_start(out=g_rows[:, 0, :], in_=g_first)
+        for c in range(1, N_GROUPS):
+            load_group(c)
+
+        make_identity(nc, identity[:])
+
+        nc.vector.memset(d_last_sb[:, NS:NA], 0.0)
+        nc.vector.tensor_scalar_mul(out=d_last_sb[:, 0:NS], in0=g_last_sb[:], scalar1=-1.0)
+        nc.sync.dma_start(out=d_last, in_=d_last_sb[:])
+
+        regroup_weight(a_raw, slice(0, NS))
+        regroup_weight(b_raw, slice(NS, NA))
+        quantise_weight(slice(0, NS))
+        quantise_weight(slice(NS, NA))
+
+        quantise_group(0, transpose_group(0))
+        nc.vector.tensor_scalar_mul(out=g_rows[0:1, 0, :], in0=g_rows[0:1, 0, :], scalar1=-1.0)
+        for c in range(N_GROUPS):
+            more = c + 1 < N_GROUPS
+            if more:
+                grouped_next = transpose_group(c + 1)
+            for i in range(GROUP):
+                if more and i == GROUP // 2:
+                    quantise_group(c + 1, grouped_next)
+                j = c * GROUP + i
+                multiply_tile(j)
+                if (j + 1) % STORE_TILES == 0:
+                    store_tiles(slice(j + 1 - STORE_TILES, j + 1))

@@ -22,6 +22,7 @@ STORE_TILES = 2
 N_GROUPS = TILES // GROUP
 WORDS = NS // 2
 N_PASS = 512
+LEAD = 2
 
 FLOPS = 2 * STEPS * NS * NA
 BYTES = 2 * NS * NA + 2 * (STEPS + 1) * NS + 4 * (STEPS + 1) * NA
@@ -40,10 +41,9 @@ def tile_constrainnet_t_kernel(tc, A, B, x0, net_input, T, grad_out, out):
     with ExitStack() as ctx:
         ctx.enter_context(tc.manual_schedule())
         keep = ctx.enter_context(tc.tile_pool(name="keep", bufs=1))
-        stage = ctx.enter_context(tc.tile_pool(name="stage", bufs=2))
-        psum_t = ctx.enter_context(tc.psum_pool(name="psum_t", bufs=2))
-        psum_a = ctx.enter_context(tc.psum_pool(name="psum_a", bufs=3))
-        psum_b = ctx.enter_context(tc.psum_pool(name="psum_b", bufs=3))
+        stage = ctx.enter_context(tc.tile_pool(name="stage", bufs=3))
+        psum_t = ctx.enter_context(tc.psum_pool(name="psum_t", bufs=3))
+        psum_m = ctx.enter_context(tc.psum_pool(name="psum_m", bufs=5))
 
         g_sb = keep.tile([P, (TILES + 1) * NS], BF16)
         g_rows = g_sb[:].rearrange("p (s k) -> p s k", k=NS)
@@ -86,7 +86,7 @@ def tile_constrainnet_t_kernel(tc, A, B, x0, net_input, T, grad_out, out):
             grouped = stage.tile([P, GROUP * P * PACK], BF16, align_bytes=64)
             grouped_words = grouped[:].bitcast(F32).rearrange("p (j r u) -> p j r u", j=GROUP, u=2)
             for half in range(GROUP // 2):
-                bank = psum_t.tile([P, 2, 2, P], F32)
+                bank = psum_t.tile([P, 2, 2, P], F32, name="bank", tag="bank")
                 for i in range(2):
                     s = c * GROUP + 2 * half + i + 1
                     for u in range(2):
@@ -105,24 +105,51 @@ def tile_constrainnet_t_kernel(tc, A, B, x0, net_input, T, grad_out, out):
                 out=g_codes[:, cols].bitcast(E5M2_X4), scales=g_scales[:, cols], in_=grouped[:]
             )
 
-        def multiply_tile(j):
+        def product(acc, j, first):
             cols = slice(j * P, (j + 1) * P)
-            acc_a = psum_a.tile([P, N_PASS], F32)
-            acc_b = psum_b.tile([P, N_PASS], F32)
-            for acc, first in ((acc_a, 0), (acc_b, NA - N_PASS)):
-                nc.tensor.matmul_mx(
-                    out=acc[:],
-                    lhsT=g_codes[:, cols].bitcast(E5M2_X4),
-                    lhsT_scale=g_scales[:, cols],
-                    rhs=ab_codes[:, first : first + N_PASS].bitcast(E4M3_X4),
-                    rhs_scale=ab_scales[:, first : first + N_PASS],
-                    start=True,
-                    stop=True,
-                )
-            nc.vector.tensor_tensor(
-                out=d_sb[:, j, 0:NS], in0=acc_a[:], in1=g_rows[:, j, :], op=mybir.AluOpType.subtract
+            nc.tensor.matmul_mx(
+                out=acc[:],
+                lhsT=g_codes[:, cols].bitcast(E5M2_X4),
+                lhsT_scale=g_scales[:, cols],
+                rhs=ab_codes[:, first : first + N_PASS].bitcast(E4M3_X4),
+                rhs_scale=ab_scales[:, first : first + N_PASS],
+                start=True,
+                stop=True,
             )
-            nc.scalar.copy(out=d_sb[:, j, NS:NA], in_=acc_b[:, N_PASS - NI : N_PASS])
+
+        def states_of_tile(j):
+            acc = psum_m.tile([P, N_PASS], F32, name="acc", tag="acc")
+            product(acc, j, 0)
+            nc.vector.tensor_tensor(
+                out=d_sb[:, j, 0:NS], in0=acc[:], in1=g_rows[:, j, :], op=mybir.AluOpType.subtract
+            )
+
+        def controls_of_tile(j):
+            acc = psum_m.tile([P, N_PASS], F32, name="acc", tag="acc")
+            product(acc, j, NA - N_PASS)
+            nc.scalar.copy(out=d_sb[:, j, NS:NA], in_=acc[:, N_PASS - NI : N_PASS])
+
+        def controls_of_group(c):
+            cols = slice(c * GROUP * P, (c + 1) * GROUP * P)
+            acc = psum_m.tile([P, N_PASS], F32, name="acc", tag="acc")
+            nc.tensor.matmul_mx(
+                out=acc[:],
+                lhsT=ab_codes[:, NS:NA].bitcast(E4M3_X4),
+                lhsT_scale=ab_scales[:, NS:NA],
+                rhs=g_codes[:, cols].bitcast(E5M2_X4),
+                rhs_scale=g_scales[:, cols],
+                start=True,
+                stop=True,
+            )
+            controls = stage.tile([P, N_PASS], F32, name="controls")
+            nc.scalar.copy(out=controls[:], in_=acc[:])
+            return controls
+
+        def turn_controls(c, controls):
+            bank = psum_t.tile([P, GROUP, NI], F32, name="bank", tag="bank")
+            for i in range(GROUP):
+                nc.tensor.transpose(bank[:, i, :], controls[:, i * P : (i + 1) * P], identity[:])
+            nc.scalar.copy(out=d_sb[:, c * GROUP : (c + 1) * GROUP, NS:NA], in_=bank[:])
 
         def store_tiles(tiles):
             nc.sync.dma_start(out=d_rows[:, tiles, :], in_=d_sb[:, tiles, :])
@@ -148,14 +175,23 @@ def tile_constrainnet_t_kernel(tc, A, B, x0, net_input, T, grad_out, out):
 
         quantise_group(0, transpose_group(0))
         nc.vector.tensor_scalar_mul(out=g_rows[0:1, 0, :], in0=g_rows[0:1, 0, :], scalar1=-1.0)
+        grouped = {1: transpose_group(1)}
         for c in range(N_GROUPS):
-            more = c + 1 < N_GROUPS
-            if more:
-                grouped_next = transpose_group(c + 1)
             for i in range(GROUP):
-                if more and i == GROUP // 2:
-                    quantise_group(c + 1, grouped_next)
                 j = c * GROUP + i
-                multiply_tile(j)
+                states_of_tile(j)
+                if c < LEAD:
+                    controls_of_tile(j)
+                if i == 1 and c < LEAD:
+                    quantise_group(c + 1, grouped.pop(c + 1))
+                if (i == GROUP - 1 and c == LEAD - 1) or (i == 1 and LEAD <= c < N_GROUPS - 2):
+                    quantise_group(c + 2, grouped.pop(c + 2))
                 if (j + 1) % STORE_TILES == 0:
                     store_tiles(slice(j + 1 - STORE_TILES, j + 1))
+            if LEAD - 1 <= c < N_GROUPS - 1:
+                controls = controls_of_group(c + 1)
+            for n in (2, 3) if c == 0 else (c + 3,):
+                if n < N_GROUPS:
+                    grouped[n] = transpose_group(n)
+            if LEAD - 1 <= c < N_GROUPS - 1:
+                turn_controls(c + 1, controls)

@@ -18,8 +18,10 @@ NA = NS + NI
 STEPS = 4096
 TILES = STEPS // P
 GROUP = 4
+SIZES = (2, 2,) + (GROUP,) * 7
+STARTS = tuple(sum(SIZES[:c]) for c in range(len(SIZES)))
 STORE_TILES = 2
-N_GROUPS = TILES // GROUP
+N_GROUPS = len(SIZES)
 WORDS = NS // 2
 N_PASS = 512
 LEAD = 2
@@ -59,15 +61,24 @@ def tile_constrainnet_t_kernel(tc, A, B, x0, net_input, T, grad_out, out):
         g_last_sb = keep.tile([1, NS], BF16)
         d_last_sb = keep.tile([1, NA], F32)
         identity = keep.tile([P, P], F32)
+        zeros = keep.tile([P, N_PASS], BF16)
+
+        def negate(out, values):
+            nc.gpsimd.tensor_scalar(
+                out=out,
+                in0=values,
+                scalar1=-1.0,
+                scalar2=0.0,
+                op0=mybir.AluOpType.mult,
+                op1=mybir.AluOpType.add,
+            )
 
         def load_weight(raw, weight):
             nc.sync.dma_start(out=raw[:], in_=weight.rearrange("(q t) n -> q t n", t=PACK))
 
         def load_group(c):
-            nc.sync.dma_start(
-                out=g_rows[:, 1 + c * GROUP : 1 + (c + 1) * GROUP, :],
-                in_=g_next[:, c * GROUP : (c + 1) * GROUP, :],
-            )
+            first, end = STARTS[c], STARTS[c] + SIZES[c]
+            nc.sync.dma_start(out=g_rows[:, 1 + first : 1 + end, :], in_=g_next[:, first:end, :])
 
         def regroup_weight(raw, cols):
             nc.vector.tensor_copy(
@@ -83,12 +94,14 @@ def tile_constrainnet_t_kernel(tc, A, B, x0, net_input, T, grad_out, out):
             )
 
         def transpose_group(c):
-            grouped = stage.tile([P, GROUP * P * PACK], BF16, align_bytes=64)
-            grouped_words = grouped[:].bitcast(F32).rearrange("p (j r u) -> p j r u", j=GROUP, u=2)
-            for half in range(GROUP // 2):
+            n = SIZES[c]
+            grouped = stage.tile([P, GROUP * P * PACK], BF16, name="grouped", align_bytes=64)
+            grouped = grouped[:, 0 : n * P * PACK]
+            grouped_words = grouped.bitcast(F32).rearrange("p (j r u) -> p j r u", j=n, u=2)
+            for half in range(n // 2):
                 bank = psum_t.tile([P, 2, 2, P], F32, name="bank", tag="bank")
                 for i in range(2):
-                    s = c * GROUP + 2 * half + i + 1
+                    s = STARTS[c] + 2 * half + i + 1
                     for u in range(2):
                         nc.tensor.transpose(
                             bank[:, i, u, :], g_words[:, s, u:WORDS:2], identity[:]
@@ -100,9 +113,9 @@ def tile_constrainnet_t_kernel(tc, A, B, x0, net_input, T, grad_out, out):
             return grouped
 
         def quantise_group(c, grouped):
-            cols = slice(c * GROUP * P, (c + 1) * GROUP * P)
+            cols = slice(STARTS[c] * P, (STARTS[c] + SIZES[c]) * P)
             nc.vector.quantize_mx(
-                out=g_codes[:, cols].bitcast(E5M2_X4), scales=g_scales[:, cols], in_=grouped[:]
+                out=g_codes[:, cols].bitcast(E5M2_X4), scales=g_scales[:, cols], in_=grouped
             )
 
         def product(acc, j, first):
@@ -130,7 +143,7 @@ def tile_constrainnet_t_kernel(tc, A, B, x0, net_input, T, grad_out, out):
             nc.scalar.copy(out=d_sb[:, j, NS:NA], in_=acc[:, N_PASS - NI : N_PASS])
 
         def controls_of_group(c):
-            cols = slice(c * GROUP * P, (c + 1) * GROUP * P)
+            cols = slice(STARTS[c] * P, (STARTS[c] + GROUP) * P)
             acc = psum_m.tile([P, N_PASS], F32, name="acc", tag="acc")
             nc.tensor.matmul_mx(
                 out=acc[:],
@@ -149,49 +162,60 @@ def tile_constrainnet_t_kernel(tc, A, B, x0, net_input, T, grad_out, out):
             bank = psum_t.tile([P, GROUP, NI], F32, name="bank", tag="bank")
             for i in range(GROUP):
                 nc.tensor.transpose(bank[:, i, :], controls[:, i * P : (i + 1) * P], identity[:])
-            nc.scalar.copy(out=d_sb[:, c * GROUP : (c + 1) * GROUP, NS:NA], in_=bank[:])
+            nc.scalar.copy(out=d_sb[:, STARTS[c] : STARTS[c] + GROUP, NS:NA], in_=bank[:])
 
         def store_tiles(tiles):
             nc.sync.dma_start(out=d_rows[:, tiles, :], in_=d_sb[:, tiles, :])
 
-        nc.sync.dma_start(out=g_last_sb[:], in_=g_last)
         load_weight(a_raw, A)
         load_group(0)
         load_weight(b_raw, B)
         nc.sync.dma_start(out=g_rows[:, 0, :], in_=g_first)
         for c in range(1, N_GROUPS):
             load_group(c)
+        nc.sync.dma_start(out=g_last_sb[:], in_=g_last)
 
         make_identity(nc, identity[:])
 
-        nc.vector.memset(d_last_sb[:, NS:NA], 0.0)
-        nc.vector.tensor_scalar_mul(out=d_last_sb[:, 0:NS], in0=g_last_sb[:], scalar1=-1.0)
-        nc.sync.dma_start(out=d_last, in_=d_last_sb[:])
+        nc.vector.memset(zeros[:], 0.0)
 
+        def warm_up(times):
+            for n in range(times):
+                acc = psum_m.tile([P, N_PASS], F32, name="acc", tag="acc")
+                nc.tensor.matmul(acc[:], lhsT=zeros[:, 0:P], rhs=zeros[:], start=True, stop=True)
+
+        warm_up(6)
+        grouped = {0: transpose_group(0)}
+        warm_up(2)
         regroup_weight(a_raw, slice(0, NS))
-        regroup_weight(b_raw, slice(NS, NA))
+        quantise_group(0, grouped.pop(0))
         quantise_weight(slice(0, NS))
+        regroup_weight(b_raw, slice(NS, NA))
         quantise_weight(slice(NS, NA))
+        negate(g_rows[0:1, 0, :], g_rows[0:1, 0, :])
+        grouped[1] = transpose_group(1)
+        grouped[2] = transpose_group(2)
+        quantise_group(1, grouped.pop(1))
 
-        quantise_group(0, transpose_group(0))
-        nc.vector.tensor_scalar_mul(out=g_rows[0:1, 0, :], in0=g_rows[0:1, 0, :], scalar1=-1.0)
-        grouped = {1: transpose_group(1)}
         for c in range(N_GROUPS):
-            for i in range(GROUP):
-                j = c * GROUP + i
+            tile_by_tile = c < LEAD or c == N_GROUPS - 1
+            if 1 <= c < N_GROUPS - 1:
+                quantise_group(c + 1, grouped.pop(c + 1))
+            for i in range(SIZES[c]):
+                j = STARTS[c] + i
                 states_of_tile(j)
-                if c < LEAD:
+                if tile_by_tile:
                     controls_of_tile(j)
-                if i == 1 and c < LEAD:
-                    quantise_group(c + 1, grouped.pop(c + 1))
-                if (i == GROUP - 1 and c == LEAD - 1) or (i == 1 and LEAD <= c < N_GROUPS - 2):
-                    quantise_group(c + 2, grouped.pop(c + 2))
+                if i == SIZES[c] // 2 - 1:
+                    if not tile_by_tile:
+                        controls = controls_of_group(c)
+                    if 1 <= c < N_GROUPS - 2:
+                        grouped[c + 2] = transpose_group(c + 2)
+                    if not tile_by_tile:
+                        turn_controls(c, controls)
                 if (j + 1) % STORE_TILES == 0:
                     store_tiles(slice(j + 1 - STORE_TILES, j + 1))
-            if LEAD - 1 <= c < N_GROUPS - 1:
-                controls = controls_of_group(c + 1)
-            for n in (2, 3) if c == 0 else (c + 3,):
-                if n < N_GROUPS:
-                    grouped[n] = transpose_group(n)
-            if LEAD - 1 <= c < N_GROUPS - 1:
-                turn_controls(c + 1, controls)
+            if c == LEAD:
+                nc.gpsimd.memset(d_last_sb[:, NS:NA], 0.0)
+                negate(d_last_sb[:, 0:NS], g_last_sb[:])
+                nc.sync.dma_start(out=d_last, in_=d_last_sb[:])

@@ -137,6 +137,17 @@ def tile_constrainnet_t_kernel(tc, A, B, x0, net_input, T, grad_out, out):
                 out=d_sb[:, j, 0:NS], in0=acc[:], in1=g_rows[:, j, :], op=mybir.AluOpType.subtract
             )
 
+        def states_of_tile_by_copy(j):
+            acc = psum_m.tile([P, N_PASS], F32, name="acc", tag="acc")
+            product(acc, j, 0)
+            nc.scalar.copy(out=d_sb[:, j, 0:NS], in_=acc[:])
+            nc.gpsimd.tensor_tensor(
+                out=d_sb[:, j, 0:NS],
+                in0=d_sb[:, j, 0:NS],
+                in1=g_rows[:, j, :],
+                op=mybir.AluOpType.subtract,
+            )
+
         def controls_of_tile(j):
             acc = psum_m.tile([P, N_PASS], F32, name="acc", tag="acc")
             product(acc, j, NA - N_PASS)
@@ -203,7 +214,10 @@ def tile_constrainnet_t_kernel(tc, A, B, x0, net_input, T, grad_out, out):
                 quantise_group(c + 1, grouped.pop(c + 1))
             for i in range(SIZES[c]):
                 j = STARTS[c] + i
-                states_of_tile(j)
+                if i == 0 and not tile_by_tile:
+                    states_of_tile_by_copy(j)
+                else:
+                    states_of_tile(j)
                 if tile_by_tile:
                     controls_of_tile(j)
                 if i == SIZES[c] // 2 - 1:

@@ -197,7 +197,7 @@ def tile_constrainnet_t_kernel(tc, A, B, x0, net_input, T, grad_out, out):
 
         warm_up(6)
         grouped = {0: transpose_group(0)}
-        warm_up(2)
+        warm_up(3)
         regroup_weight(a_raw, slice(0, NS))
         quantise_group(0, grouped.pop(0))
         quantise_weight(slice(0, NS))
@@ -212,17 +212,17 @@ def tile_constrainnet_t_kernel(tc, A, B, x0, net_input, T, grad_out, out):
             tile_by_tile = c < LEAD or c == N_GROUPS - 1
             if 1 <= c < N_GROUPS - 1:
                 quantise_group(c + 1, grouped.pop(c + 1))
+            if not tile_by_tile:
+                controls = controls_of_group(c)
             for i in range(SIZES[c]):
                 j = STARTS[c] + i
-                if i == 0 and not tile_by_tile:
+                if i == 0 and not tile_by_tile and c % 2 == 1:
                     states_of_tile_by_copy(j)
                 else:
                     states_of_tile(j)
                 if tile_by_tile:
                     controls_of_tile(j)
                 if i == SIZES[c] // 2 - 1:
-                    if not tile_by_tile:
-                        controls = controls_of_group(c)
                     if 1 <= c < N_GROUPS - 2:
                         grouped[c + 2] = transpose_group(c + 2)
                     if not tile_by_tile:

@@ -20,6 +20,7 @@ TILES = STEPS // P
 GROUP = 4
 SIZES = (2, 2,) + (GROUP,) * 7
 STARTS = tuple(sum(SIZES[:c]) for c in range(len(SIZES)))
+LOAD_ENDS = (3, 5, 9, 17, 25, TILES)
 STORE_TILES = 2
 N_GROUPS = len(SIZES)
 WORDS = NS // 2
@@ -34,8 +35,7 @@ def tile_constrainnet_t_kernel(tc, A, B, x0, net_input, T, grad_out, out):
     nc = tc.nc
     assert T == STEPS + 1
 
-    g_next = grad_out[NS : (STEPS + 1) * NS].rearrange("(p s k) -> p s k", p=P, k=NS)
-    g_first = grad_out[0 : STEPS * NS].rearrange("(p s k) -> p s k", p=P, k=NS)[:, 0, :]
+    g_own = grad_out[0 : STEPS * NS].rearrange("(p s k) -> p s k", p=P, k=NS)
     g_last = grad_out[STEPS * NS : (STEPS + 1) * NS].rearrange("(o k) -> o k", o=1)
     d_rows = out[0 : STEPS * NA].rearrange("(p j n) -> p j n", p=P, n=NA)
     d_last = out[STEPS * NA : (STEPS + 1) * NA].rearrange("(o n) -> o n", o=1)
@@ -47,7 +47,7 @@ def tile_constrainnet_t_kernel(tc, A, B, x0, net_input, T, grad_out, out):
         psum_t = ctx.enter_context(tc.psum_pool(name="psum_t", bufs=3))
         psum_m = ctx.enter_context(tc.psum_pool(name="psum_m", bufs=5))
 
-        g_sb = keep.tile([P, (TILES + 1) * NS], BF16)
+        g_sb = keep.tile([P, TILES * NS], BF16)
         g_rows = g_sb[:].rearrange("p (s k) -> p s k", k=NS)
         g_words = g_sb[:].bitcast(F32).rearrange("p (s w) -> p s w", w=WORDS)
         g_codes = keep.tile([P, TILES * P], U32, align_bytes=64)
@@ -58,9 +58,11 @@ def tile_constrainnet_t_kernel(tc, A, B, x0, net_input, T, grad_out, out):
         ab_codes = keep.tile([P, NA], U32, align_bytes=64)
         ab_scales = keep.tile([P, NA], U8, align_bytes=64)
         d_sb = keep.tile([P, TILES, NA], F32)
-        g_last_sb = keep.tile([1, NS], BF16)
+        g_edge = keep.tile([P, NS], BF16)
+        g_edge_words = g_edge[:].bitcast(F32)
         d_last_sb = keep.tile([1, NA], F32)
         identity = keep.tile([P, P], F32)
+        rotation = keep.tile([P, P], F32)
         zeros = keep.tile([P, N_PASS], BF16)
 
         def negate(out, values):
@@ -76,9 +78,9 @@ def tile_constrainnet_t_kernel(tc, A, B, x0, net_input, T, grad_out, out):
         def load_weight(raw, weight):
             nc.sync.dma_start(out=raw[:], in_=weight.rearrange("(q t) n -> q t n", t=PACK))
 
-        def load_group(c):
-            first, end = STARTS[c], STARTS[c] + SIZES[c]
-            nc.sync.dma_start(out=g_rows[:, 1 + first : 1 + end, :], in_=g_next[:, first:end, :])
+        def load_rows(first, end):
+            rows = slice(first, end)
+            nc.sync.dma_start(out=g_rows[:, rows, :], in_=g_own[:, rows, :])
 
         def regroup_weight(raw, cols):
             nc.vector.tensor_copy(
@@ -103,9 +105,11 @@ def tile_constrainnet_t_kernel(tc, A, B, x0, net_input, T, grad_out, out):
                 for i in range(2):
                     s = STARTS[c] + 2 * half + i + 1
                     for u in range(2):
-                        nc.tensor.transpose(
-                            bank[:, i, u, :], g_words[:, s, u:WORDS:2], identity[:]
-                        )
+                        if s < TILES:
+                            words, order = g_words[:, s, u:WORDS:2], identity
+                        else:
+                            words, order = g_edge_words[:, u:WORDS:2], rotation
+                        nc.tensor.transpose(bank[:, i, u, :], words, order[:])
                 nc.scalar.copy(
                     out=grouped_words[:, 2 * half : 2 * half + 2, :, :],
                     in_=bank[:].rearrange("p i u r -> p i r u"),
@@ -179,14 +183,15 @@ def tile_constrainnet_t_kernel(tc, A, B, x0, net_input, T, grad_out, out):
             nc.sync.dma_start(out=d_rows[:, tiles, :], in_=d_sb[:, tiles, :])
 
         load_weight(a_raw, A)
-        load_group(0)
+        load_rows(1, LOAD_ENDS[0])
         load_weight(b_raw, B)
-        nc.sync.dma_start(out=g_rows[:, 0, :], in_=g_first)
-        for c in range(1, N_GROUPS):
-            load_group(c)
-        nc.sync.dma_start(out=g_last_sb[:], in_=g_last)
+        load_rows(0, 1)
+        for first, end in zip(LOAD_ENDS[:-1], LOAD_ENDS[1:]):
+            load_rows(first, end)
 
         make_identity(nc, identity[:])
+        nc.gpsimd.tensor_copy(out=rotation[:, 0 : P - 1], in_=identity[:, 1:P])
+        nc.gpsimd.tensor_copy(out=rotation[:, P - 1 : P], in_=identity[:, 0:1])
 
         nc.vector.memset(zeros[:], 0.0)
 
@@ -203,6 +208,8 @@ def tile_constrainnet_t_kernel(tc, A, B, x0, net_input, T, grad_out, out):
         quantise_weight(slice(0, NS))
         regroup_weight(b_raw, slice(NS, NA))
         quantise_weight(slice(NS, NA))
+        nc.scalar.copy(out=g_edge[:], in_=g_rows[:, 0, :])
+        nc.sync.dma_start(out=g_edge[0:1, :], in_=g_last)
         negate(g_rows[0:1, 0, :], g_rows[0:1, 0, :])
         grouped[1] = transpose_group(1)
         grouped[2] = transpose_group(2)
@@ -231,5 +238,5 @@ def tile_constrainnet_t_kernel(tc, A, B, x0, net_input, T, grad_out, out):
                     store_tiles(slice(j + 1 - STORE_TILES, j + 1))
             if c == LEAD:
                 nc.gpsimd.memset(d_last_sb[:, NS:NA], 0.0)
-                negate(d_last_sb[:, 0:NS], g_last_sb[:])
+                negate(d_last_sb[:, 0:NS], g_edge[0:1, :])
                 nc.sync.dma_start(out=d_last, in_=d_last_sb[:])

@@ -20,7 +20,6 @@ TILES = STEPS // P
 GROUP = 4
 SIZES = (2, 2,) + (GROUP,) * 7
 STARTS = tuple(sum(SIZES[:c]) for c in range(len(SIZES)))
-LOAD_ENDS = (3, 5, 9, 17, 25, TILES)
 STORE_TILES = 2
 N_GROUPS = len(SIZES)
 WORDS = NS // 2
@@ -182,12 +181,14 @@ def tile_constrainnet_t_kernel(tc, A, B, x0, net_input, T, grad_out, out):
         def store_tiles(tiles):
             nc.sync.dma_start(out=d_rows[:, tiles, :], in_=d_sb[:, tiles, :])
 
+        load_rows(1, 3)
         load_weight(a_raw, A)
-        load_rows(1, LOAD_ENDS[0])
+        load_rows(3, 5)
+        load_rows(5, 9)
         load_weight(b_raw, B)
         load_rows(0, 1)
-        for first, end in zip(LOAD_ENDS[:-1], LOAD_ENDS[1:]):
-            load_rows(first, end)
+        for first in range(9, TILES, 8):
+            load_rows(first, min(first + 8, TILES))
 
         make_identity(nc, identity[:])
         nc.gpsimd.tensor_copy(out=rotation[:, 0 : P - 1], in_=identity[:, 1:P])
@@ -200,9 +201,9 @@ def tile_constrainnet_t_kernel(tc, A, B, x0, net_input, T, grad_out, out):
                 acc = psum_m.tile([P, N_PASS], F32, name="acc", tag="acc")
                 nc.tensor.matmul(acc[:], lhsT=zeros[:, 0:P], rhs=zeros[:], start=True, stop=True)
 
-        warm_up(6)
+        warm_up(4)
         grouped = {0: transpose_group(0)}
-        warm_up(3)
+        warm_up(4)
         regroup_weight(a_raw, slice(0, NS))
         quantise_group(0, grouped.pop(0))
         quantise_weight(slice(0, NS))

@@ -64,16 +64,6 @@ def tile_constrainnet_t_kernel(tc, A, B, x0, net_input, T, grad_out, out):
         rotation = keep.tile([P, P], F32)
         zeros = keep.tile([P, N_PASS], BF16)
 
-        def negate(out, values):
-            nc.gpsimd.tensor_scalar(
-                out=out,
-                in0=values,
-                scalar1=-1.0,
-                scalar2=0.0,
-                op0=mybir.AluOpType.mult,
-                op1=mybir.AluOpType.add,
-            )
-
         def load_weight(raw, weight):
             nc.sync.dma_start(out=raw[:], in_=weight.rearrange("(q t) n -> q t n", t=PACK))
 
@@ -203,18 +193,19 @@ def tile_constrainnet_t_kernel(tc, A, B, x0, net_input, T, grad_out, out):
 
         warm_up(4)
         grouped = {0: transpose_group(0)}
-        warm_up(4)
+        warm_up(3)
         regroup_weight(a_raw, slice(0, NS))
         quantise_group(0, grouped.pop(0))
         quantise_weight(slice(0, NS))
         regroup_weight(b_raw, slice(NS, NA))
         quantise_weight(slice(NS, NA))
-        nc.scalar.copy(out=g_edge[:], in_=g_rows[:, 0, :])
-        nc.sync.dma_start(out=g_edge[0:1, :], in_=g_last)
-        negate(g_rows[0:1, 0, :], g_rows[0:1, 0, :])
         grouped[1] = transpose_group(1)
+        warm_up(2)
         grouped[2] = transpose_group(2)
         quantise_group(1, grouped.pop(1))
+        nc.vector.tensor_copy(out=g_edge[:], in_=g_rows[:, 0, :])
+        nc.sync.dma_start(out=g_edge[0:1, :], in_=g_last)
+        nc.vector.tensor_scalar_mul(out=g_rows[0:1, 0, :], in0=g_rows[0:1, 0, :], scalar1=-1.0)
 
         for c in range(N_GROUPS):
             tile_by_tile = c < LEAD or c == N_GROUPS - 1
@@ -237,7 +228,14 @@ def tile_constrainnet_t_kernel(tc, A, B, x0, net_input, T, grad_out, out):
                         turn_controls(c, controls)
                 if (j + 1) % STORE_TILES == 0:
                     store_tiles(slice(j + 1 - STORE_TILES, j + 1))
-            if c == LEAD:
+            if c == N_GROUPS - 2:
                 nc.gpsimd.memset(d_last_sb[:, NS:NA], 0.0)
-                negate(d_last_sb[:, 0:NS], g_edge[0:1, :])
+                nc.gpsimd.tensor_scalar(
+                    out=d_last_sb[:, 0:NS],
+                    in0=g_edge[0:1, :],
+                    scalar1=-1.0,
+                    scalar2=0.0,
+                    op0=mybir.AluOpType.mult,
+                    op1=mybir.AluOpType.add,
+                )
                 nc.sync.dma_start(out=d_last, in_=d_last_sb[:])

from contextlib import ExitStack

import concourse.mybir as mybir
from concourse.masks import make_identity

BF16 = mybir.dt.bfloat16
F32 = mybir.dt.float32
U32 = mybir.dt.uint32
U8 = mybir.dt.uint8
E5M2_X4 = mybir.dt.float8_e5m2_x4
E4M3_X4 = mybir.dt.float8_e4m3fn_x4

P = 128
PACK = 4
NS = 512
NI = 128
NA = NS + NI
STEPS = 4096
TILES = STEPS // P
GROUP = 4
SIZES = (2, 2,) + (GROUP,) * 7
STARTS = tuple(sum(SIZES[:c]) for c in range(len(SIZES)))
STORE_TILES = 2
N_GROUPS = len(SIZES)
WORDS = NS // 2
N_PASS = 512
LEAD = 2

FLOPS = 2 * STEPS * NS * NA
BYTES = 2 * NS * NA + 2 * (STEPS + 1) * NS + 4 * (STEPS + 1) * NA


def tile_constrainnet_t_kernel(tc, A, B, x0, net_input, T, grad_out, out):
    nc = tc.nc
    assert T == STEPS + 1

    g_own = grad_out[0 : STEPS * NS].rearrange("(p s k) -> p s k", p=P, k=NS)
    g_last = grad_out[STEPS * NS : (STEPS + 1) * NS].rearrange("(o k) -> o k", o=1)
    d_rows = out[0 : STEPS * NA].rearrange("(p j n) -> p j n", p=P, n=NA)
    d_last = out[STEPS * NA : (STEPS + 1) * NA].rearrange("(o n) -> o n", o=1)

    with ExitStack() as ctx:
        ctx.enter_context(tc.manual_schedule())
        keep = ctx.enter_context(tc.tile_pool(name="keep", bufs=1))
        stage = ctx.enter_context(tc.tile_pool(name="stage", bufs=3))
        psum_t = ctx.enter_context(tc.psum_pool(name="psum_t", bufs=3))
        psum_m = ctx.enter_context(tc.psum_pool(name="psum_m", bufs=5))

        g_sb = keep.tile([P, TILES * NS], BF16)
        g_rows = g_sb[:].rearrange("p (s k) -> p s k", k=NS)
        g_words = g_sb[:].bitcast(F32).rearrange("p (s w) -> p s w", w=WORDS)
        g_codes = keep.tile([P, TILES * P], U32, align_bytes=64)
        g_scales = keep.tile([P, TILES * P], U8, align_bytes=64)
        a_raw = keep.tile([P, PACK, NS], BF16)
        b_raw = keep.tile([P, PACK, NI], BF16)
        ab_grouped = keep.tile([P, NA, PACK], BF16, align_bytes=64)
        ab_codes = keep.tile([P, NA], U32, align_bytes=64)
        ab_scales = keep.tile([P, NA], U8, align_bytes=64)
        d_sb = keep.tile([P, TILES, NA], F32)
        g_edge = keep.tile([P, NS], BF16)
        g_edge_words = g_edge[:].bitcast(F32)
        d_last_sb = keep.tile([1, NA], F32)
        identity = keep.tile([P, P], F32)
        rotation = keep.tile([P, P], F32)
        zeros = keep.tile([P, N_PASS], BF16)

        def load_weight(raw, weight):
            nc.sync.dma_start(out=raw[:], in_=weight.rearrange("(q t) n -> q t n", t=PACK))

        def load_rows(first, end):
            rows = slice(first, end)
            nc.sync.dma_start(out=g_rows[:, rows, :], in_=g_own[:, rows, :])

        def regroup_weight(raw, cols):
            nc.vector.tensor_copy(
                out=ab_grouped[:, cols, :].rearrange("p (c i) t -> p c t i", i=4),
                in_=raw[:].rearrange("p t (c i) -> p c t i", i=4),
            )

        def quantise_weight(cols):
            nc.vector.quantize_mx(
                out=ab_codes[:, cols].bitcast(E4M3_X4),
                scales=ab_scales[:, cols],
                in_=ab_grouped[:, cols, :].rearrange("p n t -> p (n t)"),
            )

        def transpose_group(c):
            n = SIZES[c]
            grouped = stage.tile([P, GROUP * P * PACK], BF16, name="grouped", align_bytes=64)
            grouped = grouped[:, 0 : n * P * PACK]
            grouped_words = grouped.bitcast(F32).rearrange("p (j r u) -> p j r u", j=n, u=2)
            for half in range(n // 2):
                bank = psum_t.tile([P, 2, 2, P], F32, name="bank", tag="bank")
                for i in range(2):
                    s = STARTS[c] + 2 * half + i + 1
                    for u in range(2):
                        if s < TILES:
                            words, order = g_words[:, s, u:WORDS:2], identity
                        else:
                            words, order = g_edge_words[:, u:WORDS:2], rotation
                        nc.tensor.transpose(bank[:, i, u, :], words, order[:])
                nc.scalar.copy(
                    out=grouped_words[:, 2 * half : 2 * half + 2, :, :],
                    in_=bank[:].rearrange("p i u r -> p i r u"),
                )
            return grouped

        def quantise_group(c, grouped):
            cols = slice(STARTS[c] * P, (STARTS[c] + SIZES[c]) * P)
            nc.vector.quantize_mx(
                out=g_codes[:, cols].bitcast(E5M2_X4), scales=g_scales[:, cols], in_=grouped
            )

        def product(acc, j, first):
            cols = slice(j * P, (j + 1) * P)
            nc.tensor.matmul_mx(
                out=acc[:],
                lhsT=g_codes[:, cols].bitcast(E5M2_X4),
                lhsT_scale=g_scales[:, cols],
                rhs=ab_codes[:, first : first + N_PASS].bitcast(E4M3_X4),
                rhs_scale=ab_scales[:, first : first + N_PASS],
                start=True,
                stop=True,
            )

        def states_of_tile(j):
            acc = psum_m.tile([P, N_PASS], F32, name="acc", tag="acc")
            product(acc, j, 0)
            nc.vector.tensor_tensor(
                out=d_sb[:, j, 0:NS], in0=acc[:], in1=g_rows[:, j, :], op=mybir.AluOpType.subtract
            )

        def states_of_tile_by_copy(j):
            acc = psum_m.tile([P, N_PASS], F32, name="acc", tag="acc")
            product(acc, j, 0)
            nc.scalar.copy(out=d_sb[:, j, 0:NS], in_=acc[:])
            nc.gpsimd.tensor_tensor(
                out=d_sb[:, j, 0:NS],
                in0=d_sb[:, j, 0:NS],
                in1=g_rows[:, j, :],
                op=mybir.AluOpType.subtract,
            )

        def controls_of_tile(j):
            acc = psum_m.tile([P, N_PASS], F32, name="acc", tag="acc")
            product(acc, j, NA - N_PASS)
            nc.scalar.copy(out=d_sb[:, j, NS:NA], in_=acc[:, N_PASS - NI : N_PASS])

        def controls_of_group(c):
            cols = slice(STARTS[c] * P, (STARTS[c] + GROUP) * P)
            acc = psum_m.tile([P, N_PASS], F32, name="acc", tag="acc")
            nc.tensor.matmul_mx(
                out=acc[:],
                lhsT=ab_codes[:, NS:NA].bitcast(E4M3_X4),
                lhsT_scale=ab_scales[:, NS:NA],
                rhs=g_codes[:, cols].bitcast(E5M2_X4),
                rhs_scale=g_scales[:, cols],
                start=True,
                stop=True,
            )
            controls = stage.tile([P, N_PASS], F32, name="controls")
            nc.scalar.copy(out=controls[:], in_=acc[:])
            return controls

        def turn_controls(c, controls):
            bank = psum_t.tile([P, GROUP, NI], F32, name="bank", tag="bank")
            for i in range(GROUP):
                nc.tensor.transpose(bank[:, i, :], controls[:, i * P : (i + 1) * P], identity[:])
            nc.scalar.copy(out=d_sb[:, STARTS[c] : STARTS[c] + GROUP, NS:NA], in_=bank[:])

        def store_tiles(tiles):
            nc.sync.dma_start(out=d_rows[:, tiles, :], in_=d_sb[:, tiles, :])

        load_rows(1, 3)
        load_weight(a_raw, A)
        load_rows(3, 5)
        load_rows(5, 9)
        load_weight(b_raw, B)
        load_rows(0, 1)
        for first in range(9, TILES, 8):
            load_rows(first, min(first + 8, TILES))

        make_identity(nc, identity[:])
        nc.gpsimd.tensor_copy(out=rotation[:, 0 : P - 1], in_=identity[:, 1:P])
        nc.gpsimd.tensor_copy(out=rotation[:, P - 1 : P], in_=identity[:, 0:1])

        nc.vector.memset(zeros[:], 0.0)

        def warm_up(times):
            for n in range(times):
                acc = psum_m.tile([P, N_PASS], F32, name="acc", tag="acc")
                nc.tensor.matmul(acc[:], lhsT=zeros[:, 0:P], rhs=zeros[:], start=True, stop=True)

        warm_up(4)
        grouped = {0: transpose_group(0)}
        warm_up(3)
        regroup_weight(a_raw, slice(0, NS))
        quantise_group(0, grouped.pop(0))
        quantise_weight(slice(0, NS))
        regroup_weight(b_raw, slice(NS, NA))
        quantise_weight(slice(NS, NA))
        grouped[1] = transpose_group(1)
        warm_up(2)
        grouped[2] = transpose_group(2)
        quantise_group(1, grouped.pop(1))
        nc.vector.tensor_copy(out=g_edge[:], in_=g_rows[:, 0, :])
        nc.sync.dma_start(out=g_edge[0:1, :], in_=g_last)
        nc.vector.tensor_scalar_mul(out=g_rows[0:1, 0, :], in0=g_rows[0:1, 0, :], scalar1=-1.0)

        for c in range(N_GROUPS):
            tile_by_tile = c < LEAD or c == N_GROUPS - 1
            if 1 <= c < N_GROUPS - 1:
                quantise_group(c + 1, grouped.pop(c + 1))
            if not tile_by_tile:
                controls = controls_of_group(c)
            for i in range(SIZES[c]):
                j = STARTS[c] + i
                if i == 0 and not tile_by_tile and c % 2 == 1:
                    states_of_tile_by_copy(j)
                else:
                    states_of_tile(j)
                if tile_by_tile:
                    controls_of_tile(j)
                if i == SIZES[c] // 2 - 1:
                    if 1 <= c < N_GROUPS - 2:
                        grouped[c + 2] = transpose_group(c + 2)
                    if not tile_by_tile:
                        turn_controls(c, controls)
                if (j + 1) % STORE_TILES == 0:
                    store_tiles(slice(j + 1 - STORE_TILES, j + 1))
            if c == N_GROUPS - 2:
                nc.gpsimd.memset(d_last_sb[:, NS:NA], 0.0)
                nc.gpsimd.tensor_scalar(
                    out=d_last_sb[:, 0:NS],
                    in0=g_edge[0:1, :],
                    scalar1=-1.0,
                    scalar2=0.0,
                    op0=mybir.AluOpType.mult,
                    op1=mybir.AluOpType.add,
                )
                nc.sync.dma_start(out=d_last, in_=d_last_sb[:])
